import numpy as np
import ml_dtypes


def mxq(x, axis, fmt="e4m3"):
    dtype, down = {"e4m3": (ml_dtypes.float8_e4m3fn, 7), "e5m2": (ml_dtypes.float8_e5m2, 14)}[fmt]
    v = np.moveaxis(np.asarray(x, np.float32).astype(ml_dtypes.bfloat16).astype(np.float64), axis, -1)
    blocks = v.reshape(v.shape[:-1] + (-1, 32))
    amax = np.abs(blocks).max(-1, keepdims=True)
    byte = np.maximum(np.where(amax > 0, np.frexp(amax)[1] - 1 + 127, 0) - down, 1)
    scale = np.exp2(byte - 127.0)
    codes = (blocks / scale).astype(np.float32).astype(dtype).astype(np.float64)
    return np.moveaxis((codes * scale).reshape(v.shape), -1, axis)


WIDE = False


def mx_kscale(k):
    if not WIDE:
        return np.ones(k)
    levels = np.array([10, -10, 5, -5, 0])
    a = np.random.permutation(np.resize(levels, k // 512 * 4)).reshape(k // 512, 4)
    idx = np.arange(k)
    return np.exp2(a[idx // 512, idx % 128 // 32])


BF16 = ml_dtypes.bfloat16


def bf(x):
    return np.asarray(x, np.float32).astype(BF16)


def f64(x):
    return np.asarray(x).astype(np.float64)


E2M1 = np.array([0.0, 0.5, 1.0, 1.5, 2.0, 3.0, 4.0, 6.0, -0.0, -0.5, -1.0, -1.5, -2.0, -3.0, -4.0, -6.0])


def pack_weight(w, fmt):
    k, n = w.shape
    w = f64(bf(w)).reshape(k // 32, 32, n)
    amax = np.abs(w).max(1)
    if fmt == "e4m3":
        byte = np.frexp(amax)[1] - 1 + 127 - 7
    else:
        mant, ex = np.frexp(amax / 6.0)
        byte = np.where(mant > 0.5, ex, ex - 1) + 127
    byte = np.clip(np.where(amax > 0, byte, 1), 1, 254)
    scaled = (w * np.exp2(127.0 - byte)[:, None, :]).reshape(k, n).astype(np.float32)
    by_word = np.ascontiguousarray(scaled.reshape(k // 512, 128, 4, n).transpose(0, 1, 3, 2))
    if fmt == "e4m3":
        words = by_word.astype(ml_dtypes.float8_e4m3fn).view(np.uint8)
    else:
        c = by_word.astype(ml_dtypes.float4_e2m1fn).view(np.uint8) & 0xF
        words = c[..., 0::2] | (c[..., 1::2] << 4)
    return np.ascontiguousarray(words), np.ascontiguousarray(byte.astype(np.uint8).reshape(k // 512, 16, n))


def unpack_weight(words, scales, fmt):
    g, p, n, _ = words.shape
    if fmt == "e4m3":
        vals = np.ascontiguousarray(words).view(ml_dtypes.float8_e4m3fn).astype(np.float64)
    else:
        nib = np.empty((g, p, n, 4), np.uint8)
        nib[..., 0::2] = words & 0xF
        nib[..., 1::2] = words >> 4
        vals = E2M1[nib]
    vals = vals * np.repeat(np.exp2(scales.astype(np.float64) - 127.0), 8, axis=1)[..., None]
    return vals.transpose(0, 1, 3, 2).reshape(g * 512, n)


N, IN_DIM, HID, NUM_CLASSES, AVG_DEG = 1024, 8192, 512, 512, 32


def setup_inputs():
    s = mx_kscale(IN_DIM)
    edges = np.random.uniform(size=(N, N)) < AVG_DEG / N
    A = bf(edges * (0.5 + np.random.uniform(size=(N, N))))
    x = bf(np.random.standard_normal((N, IN_DIM)) * 0.5 * s)
    W1_words, W1_scales = pack_weight(np.random.standard_normal((IN_DIM, HID)) * 4.0 / np.sqrt(IN_DIM) / s[:, None], "e4m3")
    b1 = bf(np.random.standard_normal(HID) * 0.1)
    return {"A": A,
            "x": x,
            "W1_words": W1_words,
            "W1_scales": W1_scales,
            "b1": b1}


def reference(A, x, W1_words, W1_scales, b1):
    A = f64(A)
    deg = A.sum(0) + 1.0
    dis = (1.0 / np.sqrt(deg))[:, None]
    h = mxq(f64(x), 1, "e4m3") @ unpack_weight(W1_words, W1_scales, "e4m3")
    m = dis * h
    agg = mxq(A, 0, "e4m3").T @ mxq(m, 0, "e4m3")
    return np.maximum(dis * agg + dis ** 2 * h + f64(b1), 0.0)

@@ -1,0 +1,290 @@
+from contextlib import ExitStack
+
+import concourse.masks as masks
+import concourse.mybir as mybir
+
+F32 = mybir.dt.float32
+BF16 = mybir.dt.bfloat16
+I32 = mybir.dt.int32
+U32 = mybir.dt.uint32
+U8 = mybir.dt.uint8
+FP8X4 = mybir.dt.float8_e4m3fn_x4
+ACT = mybir.ActivationFunctionType
+ALU = mybir.AluOpType
+
+P = 128
+PACK = 4
+K_PASS = P * PACK
+NODES = 1024
+FEATURES = 8192
+HIDDEN = 512
+
+ROW_TILES = NODES // P
+TILES_PER_HALF = PACK
+HALVES = ROW_TILES // TILES_PER_HALF
+TILES_PER_STEP = 2
+PASSES_PER_CHUNK = 4
+K_CHUNK = PASSES_PER_CHUNK * K_PASS
+CHUNKS = FEATURES // K_CHUNK
+STEPS_PER_CHUNK = TILES_PER_HALF // TILES_PER_STEP
+STEPS_PER_HALF = CHUNKS * STEPS_PER_CHUNK
+STEPS = HALVES * STEPS_PER_HALF
+WORDS_PER_PASS = K_PASS // 2
+PASSES_PER_BANK = 2
+LOADS_AHEAD = 6
+DEG_COLS = 32
+A_PIECE = 256
+A_PIECES = HALVES * NODES // A_PIECE
+
+FLOPS = 2 * NODES * FEATURES * HIDDEN + 2 * NODES * NODES * HIDDEN
+
+
+def tile_gcnnodeclassifiernetwork_pa_k_kernel(tc, A, x, W1_words, W1_scales, b1, out):
+    nc = tc.nc
+    with ExitStack() as ctx:
+        keep = ctx.enter_context(tc.tile_pool(name="keep", bufs=1))
+        x_pool = ctx.enter_context(tc.tile_pool(name="x", bufs=LOADS_AHEAD))
+        stage = ctx.enter_context(tc.tile_pool(name="stage", bufs=2))
+        out_pool = ctx.enter_context(tc.tile_pool(name="out", bufs=4))
+        acc_pool = ctx.enter_context(tc.psum_pool(name="acc", bufs=1))
+        bank_pool = ctx.enter_context(tc.psum_pool(name="bank", bufs=4))
+        ctx.enter_context(tc.manual_schedule())
+
+        w_words = keep.tile([P, CHUNKS * PASSES_PER_CHUNK, HIDDEN], U32, align_bytes=64)
+        w_planes = keep.tile([P, CHUNKS, HIDDEN], U8, align_bytes=64)
+        a_raw = keep.tile([P, HALVES, PACK, NODES], BF16)
+        a_codes = keep.tile([P, HALVES, NODES], U32, align_bytes=64)
+        a_scales = keep.tile([P, HALVES, NODES], U8, align_bytes=64)
+        m_codes = keep.tile([P, HALVES, HIDDEN], U32, align_bytes=64)
+        m_scales = keep.tile([P, HALVES, HIDDEN], U8, align_bytes=64)
+        self_term = keep.tile([P, ROW_TILES, HIDDEN], F32)
+        bias_all = keep.tile([P, HIDDEN], F32)
+        bias_rows = keep.tile([P, HIDDEN], BF16)
+        ones = keep.tile([P, P], BF16)
+        ident = keep.tile([P, P], F32)
+        deg = keep.tile([P, ROW_TILES], F32)
+        d_sq = keep.tile([P, ROW_TILES], F32)
+        d = keep.tile([P, ROW_TILES], F32)
+
+        x_tiles = {}
+        sorted_tiles = {}
+        grouped_tiles = {}
+        x_codes = {}
+        x_scales = {}
+        a_grouped = {}
+        acc = {}
+        m_rows = {}
+
+        def place(step):
+            half, rest = divmod(step, STEPS_PER_HALF)
+            chunk, pair = divmod(rest, STEPS_PER_CHUNK)
+            return half, chunk, pair * TILES_PER_STEP
+
+        def load(step):
+            half, chunk, first = place(step)
+            x_tile = x_pool.tile([P, TILES_PER_STEP, K_CHUNK], BF16)
+            x_tiles[step] = x_tile
+            for t in range(TILES_PER_STEP):
+                row = (half * TILES_PER_HALF + first + t) * P
+                nc.sync.dma_start(
+                    out=x_tile[:, t, :],
+                    in_=x[row : row + P, chunk * K_CHUNK : (chunk + 1) * K_CHUNK],
+                )
+            if half == 0 and first + TILES_PER_STEP == TILES_PER_HALF:
+                passes = slice(chunk * PASSES_PER_CHUNK, (chunk + 1) * PASSES_PER_CHUNK)
+                for quad in range(4):
+                    nc.sync.dma_start(
+                        out=w_planes[32 * quad : 32 * quad + 16, chunk, :].bitcast(I32),
+                        in_=W1_scales[passes, 4 * quad : 4 * quad + 4, :].bitcast(I32),
+                    )
+                nc.sync.dma_start(
+                    out=w_words[:, passes, :].bitcast(I32),
+                    in_=W1_words[passes].rearrange("g p n t -> p g (n t)").bitcast(I32),
+                )
+            if step == STEPS_PER_HALF - 1:
+                for g in range(HALVES):
+                    nc.sync.dma_start(
+                        out=a_raw[:, g],
+                        in_=A.rearrange("(g t p) j -> g p t j", t=PACK, p=P)[g],
+                    )
+
+        def sort_words(step):
+            words = stage.tile([P, TILES_PER_STEP, PASSES_PER_CHUNK, 2, P], F32)
+            sorted_tiles[step] = words
+            for t in range(TILES_PER_STEP):
+                nc.vector.tensor_copy(
+                    out=words[:, t],
+                    in_=x_tiles[step][:, t, :]
+                    .bitcast(F32)
+                    .rearrange("p (g q u) -> p g u q", g=PASSES_PER_CHUNK, u=2),
+                )
+
+        def transpose(step):
+            grouped = stage.tile(
+                [P, TILES_PER_STEP, PASSES_PER_CHUNK, P, PACK], BF16, align_bytes=64
+            )
+            grouped_tiles[step] = grouped
+            for t in range(TILES_PER_STEP):
+                for g0 in range(0, PASSES_PER_CHUNK, PASSES_PER_BANK):
+                    flipped = bank_pool.tile([P, PASSES_PER_BANK, 2, P], F32, tag="bank")
+                    for g in range(PASSES_PER_BANK):
+                        for u in range(2):
+                            nc.tensor.transpose(
+                                flipped[:, g, u, :], sorted_tiles[step][:, t, g0 + g, u, :], ident[:]
+                            )
+                    nc.scalar.copy(
+                        out=grouped[:, t, g0 : g0 + PASSES_PER_BANK].bitcast(F32),
+                        in_=flipped[:].rearrange("p g u r -> p g r u"),
+                    )
+
+        def quantise(step):
+            codes = stage.tile([P, TILES_PER_STEP, PASSES_PER_CHUNK, P], U32, align_bytes=64)
+            scales = stage.tile([P, TILES_PER_STEP, PASSES_PER_CHUNK, P], U8, align_bytes=64)
+            x_codes[step] = codes
+            x_scales[step] = scales
+            for t in range(TILES_PER_STEP):
+                nc.vector.quantize_mx(
+                    out=codes[:, t].rearrange("p g r -> p (g r)").bitcast(FP8X4),
+                    scales=scales[:, t].rearrange("p g r -> p (g r)"),
+                    in_=grouped_tiles[step][:, t].rearrange("p g r k -> p (g r k)"),
+                )
+
+        def multiply(step):
+            half, chunk, first = place(step)
+            for t in range(TILES_PER_STEP):
+                if chunk == 0:
+                    acc[first + t] = acc_pool.tile(
+                        [P, HIDDEN], F32, name="acc%d" % (first + t), tag="acc%d" % (first + t)
+                    )
+                for o in range(PASSES_PER_CHUNK):
+                    nc.tensor.matmul_mx(
+                        out=acc[first + t][:],
+                        lhsT=x_codes[step][:, t, o, :].bitcast(FP8X4),
+                        lhsT_scale=x_scales[step][:, t, o, :],
+                        rhs=w_words[:, chunk * PASSES_PER_CHUNK + o, :].bitcast(FP8X4),
+                        rhs_scale=w_planes[4 * o : P, chunk, :],
+                        start=(chunk == 0 and o == 0),
+                        stop=(chunk == CHUNKS - 1 and o == PASSES_PER_CHUNK - 1),
+                    )
+
+        def degrees():
+            sums = bank_pool.tile([P, ROW_TILES, DEG_COLS], F32, tag="bank")
+            for j in range(ROW_TILES):
+                for i in range(ROW_TILES):
+                    nc.tensor.matmul(
+                        out=sums[:, j, :],
+                        lhsT=a_raw[:, i // PACK, i % PACK, j * P : (j + 1) * P],
+                        rhs=ones[:, :DEG_COLS],
+                        start=(i == 0),
+                        stop=(i == ROW_TILES - 1),
+                    )
+            nc.vector.tensor_scalar_add(out=deg[:], in0=sums[:, :, 0], scalar1=1.0)
+            nc.vector.reciprocal(out=d_sq[:], in_=deg[:])
+            nc.scalar.activation(out=d[:], in_=d_sq[:], func=ACT.Sqrt)
+
+        def empty_accumulators(step):
+            half, chunk, first = place(step)
+            if first == 0:
+                m_rows[half] = stage.tile([P, TILES_PER_HALF, HIDDEN], BF16, name="m_rows")
+            r0 = half * TILES_PER_HALF + first
+            nc.scalar.activation(
+                out=m_rows[half][:, first, :], in_=acc[first][:], func=ACT.Copy, scale=d[:, r0 : r0 + 1]
+            )
+            nc.vector.tensor_scalar_mul(
+                out=m_rows[half][:, first + 1, :], in0=acc[first + 1][:], scalar1=d[:, r0 + 1 : r0 + 2]
+            )
+            for t in range(TILES_PER_STEP):
+                nc.vector.scalar_tensor_tensor(
+                    out=self_term[:, r0 + t, :],
+                    in0=acc[first + t][:],
+                    scalar=d_sq[:, r0 + t : r0 + t + 1],
+                    in1=bias_all[:],
+                    op0=ALU.mult,
+                    op1=ALU.add,
+                )
+
+        def quantise_m(half):
+            m_grouped = stage.tile([P, HIDDEN, PACK], BF16, align_bytes=64)
+            nc.vector.tensor_copy(out=m_grouped[:], in_=m_rows[half][:].rearrange("p t c -> p c t"))
+            nc.vector.quantize_mx(
+                out=m_codes[:, half, :].bitcast(FP8X4),
+                scales=m_scales[:, half, :],
+                in_=m_grouped[:].rearrange("p c t -> p (c t)"),
+            )
+
+        def a_columns(piece):
+            g, part = divmod(piece, A_PIECES // HALVES)
+            return g, slice(part * A_PIECE, (part + 1) * A_PIECE)
+
+        def regroup_a(piece):
+            g, cols = a_columns(piece)
+            a_grouped[piece] = stage.tile([P, A_PIECE, PACK], BF16, name="a_grouped", align_bytes=64)
+            nc.scalar.copy(out=a_grouped[piece][:], in_=a_raw[:, g, :, cols].rearrange("p t j -> p j t"))
+
+        def quantise_a(piece):
+            g, cols = a_columns(piece)
+            nc.vector.quantize_mx(
+                out=a_codes[:, g, cols].bitcast(FP8X4),
+                scales=a_scales[:, g, cols],
+                in_=a_grouped[piece][:].rearrange("p j t -> p (j t)"),
+            )
+
+        nc.vector.memset(w_planes[:].bitcast(I32), 0)
+        nc.vector.memset(bias_rows[:], 0.0)
+        nc.vector.memset(ones[:], 1.0)
+        masks.make_identity(nc, ident[:])
+        nc.sync.dma_start(out=bias_rows[0:1, :], in_=b1.unsqueeze(0))
+        for step in range(LOADS_AHEAD):
+            load(step)
+        bias_bank = bank_pool.tile([P, HIDDEN], F32, tag="bank")
+        nc.tensor.matmul(out=bias_bank[:], lhsT=ones[:], rhs=bias_rows[:], start=True, stop=True)
+        nc.scalar.copy(out=bias_all[:], in_=bias_bank[:])
+        sort_words(0)
+
+        for step in range(STEPS + 1):
+            if step + LOADS_AHEAD < STEPS:
+                load(step + LOADS_AHEAD)
+            if step + 1 < STEPS:
+                sort_words(step + 1)
+            if step < STEPS:
+                transpose(step)
+            piece = step - STEPS_PER_HALF
+            if 0 <= piece < A_PIECES:
+                regroup_a(piece)
+            if 0 <= piece - 1 < A_PIECES:
+                quantise_a(piece - 1)
+            if step < STEPS:
+                quantise(step)
+            if step >= 1:
+                multiply(step - 1)
+                half, chunk, first = place(step - 1)
+                if chunk == CHUNKS - 1:
+                    if half == 0 and first == 0:
+                        degrees()
+                    empty_accumulators(step - 1)
+                    if first + TILES_PER_STEP == TILES_PER_HALF:
+                        quantise_m(half)
+
+        for j in range(ROW_TILES):
+            agg = bank_pool.tile([P, HIDDEN], F32, tag="bank")
+            for g in range(HALVES):
+                nc.tensor.matmul_mx(
+                    out=agg[:],
+                    lhsT=a_codes[:, g, j * P : (j + 1) * P].bitcast(FP8X4),
+                    lhsT_scale=a_scales[:, g, j * P : (j + 1) * P],
+                    rhs=m_codes[:, g, :].bitcast(FP8X4),
+                    rhs_scale=m_scales[:, g, :],
+                    start=(g == 0),
+                    stop=(g == HALVES - 1),
+                )
+            result = out_pool.tile([P, HIDDEN], F32)
+            nc.vector.scalar_tensor_tensor(
+                out=result[:],
+                in0=agg[:],
+                scalar=d[:, j : j + 1],
+                in1=self_term[:, j, :],
+                op0=ALU.mult,
+                op1=ALU.add,
+            )
+            nc.scalar.activation(out=result[:], in_=result[:], func=ACT.Relu)
+            nc.sync.dma_start(out=out[j * P : (j + 1) * P, :], in_=result[:])

@@ -35,6 +35,7 @@ LOADS_AHEAD = 6
 DEG_COLS = 32
 A_PIECE = 256
 A_PIECES = HALVES * NODES // A_PIECE
+A_BUFFERS = 4
 
 FLOPS = 2 * NODES * FEATURES * HIDDEN + 2 * NODES * NODES * HIDDEN
 
@@ -45,6 +46,7 @@ def tile_gcnnodeclassifiernetwork_pa_k_kernel(tc, A, x, W1_words, W1_scales, b1,
         keep = ctx.enter_context(tc.tile_pool(name="keep", bufs=1))
         x_pool = ctx.enter_context(tc.tile_pool(name="x", bufs=LOADS_AHEAD))
         stage = ctx.enter_context(tc.tile_pool(name="stage", bufs=2))
+        a_pool = ctx.enter_context(tc.tile_pool(name="a", bufs=A_BUFFERS))
         out_pool = ctx.enter_context(tc.tile_pool(name="out", bufs=4))
         acc_pool = ctx.enter_context(tc.psum_pool(name="acc", bufs=1))
         bank_pool = ctx.enter_context(tc.psum_pool(name="bank", bufs=4))
@@ -101,12 +103,6 @@ def tile_gcnnodeclassifiernetwork_pa_k_kernel(tc, A, x, W1_words, W1_scales, b1,
                     out=w_words[:, passes, :].bitcast(I32),
                     in_=W1_words[passes].rearrange("g p n t -> p g (n t)").bitcast(I32),
                 )
-            if step == STEPS_PER_HALF - 1:
-                for g in range(HALVES):
-                    nc.sync.dma_start(
-                        out=a_raw[:, g],
-                        in_=A.rearrange("(g t p) j -> g p t j", t=PACK, p=P)[g],
-                    )
 
         def sort_words(step):
             words = stage.tile([P, TILES_PER_STEP, PASSES_PER_CHUNK, 2, P], F32)
@@ -167,8 +163,7 @@ def tile_gcnnodeclassifiernetwork_pa_k_kernel(tc, A, x, W1_words, W1_scales, b1,
                         stop=(chunk == CHUNKS - 1 and o == PASSES_PER_CHUNK - 1),
                     )
 
-        def degrees():
-            sums = bank_pool.tile([P, ROW_TILES, DEG_COLS], F32, tag="bank")
+        def sum_columns(sums):
             for j in range(ROW_TILES):
                 for i in range(ROW_TILES):
                     nc.tensor.matmul(
@@ -178,6 +173,8 @@ def tile_gcnnodeclassifiernetwork_pa_k_kernel(tc, A, x, W1_words, W1_scales, b1,
                         start=(i == 0),
                         stop=(i == ROW_TILES - 1),
                     )
+
+        def normalisers(sums):
             nc.vector.tensor_scalar_add(out=deg[:], in0=sums[:, :, 0], scalar1=1.0)
             nc.vector.reciprocal(out=d_sq[:], in_=deg[:])
             nc.scalar.activation(out=d[:], in_=d_sq[:], func=ACT.Sqrt)
@@ -218,8 +215,12 @@ def tile_gcnnodeclassifiernetwork_pa_k_kernel(tc, A, x, W1_words, W1_scales, b1,
 
         def regroup_a(piece):
             g, cols = a_columns(piece)
-            a_grouped[piece] = stage.tile([P, A_PIECE, PACK], BF16, name="a_grouped", align_bytes=64)
-            nc.scalar.copy(out=a_grouped[piece][:], in_=a_raw[:, g, :, cols].rearrange("p t j -> p j t"))
+            a_grouped[piece] = a_pool.tile([P, A_PIECE, PACK], BF16, name="a_grouped", align_bytes=64)
+            rows_side_by_side = a_raw[:, g, :, cols].rearrange("p t j -> p j t")
+            if piece % 2 == 0:
+                nc.vector.tensor_copy(out=a_grouped[piece][:], in_=rows_side_by_side)
+            else:
+                nc.scalar.copy(out=a_grouped[piece][:], in_=rows_side_by_side)
 
         def quantise_a(piece):
             g, cols = a_columns(piece)
@@ -234,12 +235,24 @@ def tile_gcnnodeclassifiernetwork_pa_k_kernel(tc, A, x, W1_words, W1_scales, b1,
         nc.vector.memset(ones[:], 1.0)
         masks.make_identity(nc, ident[:])
         nc.sync.dma_start(out=bias_rows[0:1, :], in_=b1.unsqueeze(0))
+        for g in range(HALVES):
+            nc.sync.dma_start(
+                out=a_raw[:, g], in_=A.rearrange("(g t p) j -> g p t j", t=PACK, p=P)[g]
+            )
         for step in range(LOADS_AHEAD):
             load(step)
         bias_bank = bank_pool.tile([P, HIDDEN], F32, tag="bank")
         nc.tensor.matmul(out=bias_bank[:], lhsT=ones[:], rhs=bias_rows[:], start=True, stop=True)
         nc.scalar.copy(out=bias_all[:], in_=bias_bank[:])
+        for piece in range(A_PIECES + 2):
+            if piece < A_PIECES:
+                regroup_a(piece)
+            if piece >= 2:
+                quantise_a(piece - 2)
+        column_sums = bank_pool.tile([P, ROW_TILES, DEG_COLS], F32, tag="bank")
+        sum_columns(column_sums)
         sort_words(0)
+        normalisers(column_sums)
 
         for step in range(STEPS + 1):
             if step + LOADS_AHEAD < STEPS:
@@ -248,19 +261,12 @@ def tile_gcnnodeclassifiernetwork_pa_k_kernel(tc, A, x, W1_words, W1_scales, b1,
                 sort_words(step + 1)
             if step < STEPS:
                 transpose(step)
-            piece = step - STEPS_PER_HALF
-            if 0 <= piece < A_PIECES:
-                regroup_a(piece)
-            if 0 <= piece - 1 < A_PIECES:
-                quantise_a(piece - 1)
             if step < STEPS:
                 quantise(step)
             if step >= 1:
                 multiply(step - 1)
                 half, chunk, first = place(step - 1)
                 if chunk == CHUNKS - 1:
-                    if half == 0 and first == 0:
-                        degrees()
                     empty_accumulators(step - 1)
                     if first + TILES_PER_STEP == TILES_PER_HALF:
                         quantise_m(half)

@@ -31,10 +31,13 @@ STEPS_PER_HALF = CHUNKS * STEPS_PER_CHUNK
 STEPS = HALVES * STEPS_PER_HALF
 WORDS_PER_PASS = K_PASS // 2
 PASSES_PER_BANK = 2
-LOADS_AHEAD = 6
+LOADS_AHEAD = 8
 DEG_COLS = 32
 A_PIECE = 256
 A_PIECES = HALVES * NODES // A_PIECE
+SUMS_STEP = 9
+M_SPLIT = 336
+EARLY_TILES = 6
 A_BUFFERS = 4
 
 FLOPS = 2 * NODES * FEATURES * HIDDEN + 2 * NODES * NODES * HIDDEN
@@ -47,7 +50,7 @@ def tile_gcnnodeclassifiernetwork_pa_k_kernel(tc, A, x, W1_words, W1_scales, b1,
         x_pool = ctx.enter_context(tc.tile_pool(name="x", bufs=LOADS_AHEAD))
         stage = ctx.enter_context(tc.tile_pool(name="stage", bufs=2))
         a_pool = ctx.enter_context(tc.tile_pool(name="a", bufs=A_BUFFERS))
-        out_pool = ctx.enter_context(tc.tile_pool(name="out", bufs=4))
+        out_pool = ctx.enter_context(tc.tile_pool(name="out", bufs=ROW_TILES))
         acc_pool = ctx.enter_context(tc.psum_pool(name="acc", bufs=1))
         bank_pool = ctx.enter_context(tc.psum_pool(name="bank", bufs=4))
         ctx.enter_context(tc.manual_schedule())
@@ -184,25 +187,50 @@ def tile_gcnnodeclassifiernetwork_pa_k_kernel(tc, A, x, W1_words, W1_scales, b1,
             if first == 0:
                 m_rows[half] = stage.tile([P, TILES_PER_HALF, HIDDEN], BF16, name="m_rows")
             r0 = half * TILES_PER_HALF + first
+            if half == 0:
+                nc.scalar.copy(out=self_term[:, r0, :], in_=acc[first][:])
+                nc.vector.tensor_copy(out=self_term[:, r0 + 1, :], in_=acc[first + 1][:])
+                return
             nc.scalar.activation(
                 out=m_rows[half][:, first, :], in_=acc[first][:], func=ACT.Copy, scale=d[:, r0 : r0 + 1]
             )
+            self_from_acc(first)
             nc.vector.tensor_scalar_mul(
                 out=m_rows[half][:, first + 1, :], in0=acc[first + 1][:], scalar1=d[:, r0 + 1 : r0 + 2]
             )
-            for t in range(TILES_PER_STEP):
-                nc.vector.scalar_tensor_tensor(
-                    out=self_term[:, r0 + t, :],
-                    in0=acc[first + t][:],
-                    scalar=d_sq[:, r0 + t : r0 + t + 1],
-                    in1=bias_all[:],
-                    op0=ALU.mult,
-                    op1=ALU.add,
-                )
+            if first + TILES_PER_STEP == TILES_PER_HALF:
+                quantise_m(half)
+            self_from_acc(first + 1)
+
+        def self_from_acc(t):
+            r = TILES_PER_HALF + t
+            nc.vector.scalar_tensor_tensor(
+                out=self_term[:, r, :],
+                in0=acc[t][:],
+                scalar=d_sq[:, r : r + 1],
+                in1=bias_all[:],
+                op0=ALU.mult,
+                op1=ALU.add,
+            )
+
+        def scale_kept_h(r):
+            nc.scalar.activation(
+                out=m_rows[0][:, r, :], in_=self_term[:, r, :], func=ACT.Copy, scale=d[:, r : r + 1]
+            )
+            nc.vector.scalar_tensor_tensor(
+                out=self_term[:, r, :],
+                in0=self_term[:, r, :],
+                scalar=d_sq[:, r : r + 1],
+                in1=bias_all[:],
+                op0=ALU.mult,
+                op1=ALU.add,
+            )
 
         def quantise_m(half):
             m_grouped = stage.tile([P, HIDDEN, PACK], BF16, align_bytes=64)
-            nc.vector.tensor_copy(out=m_grouped[:], in_=m_rows[half][:].rearrange("p t c -> p c t"))
+            rows_side_by_side = m_rows[half][:].rearrange("p t c -> p c t")
+            nc.scalar.copy(out=m_grouped[:, M_SPLIT:, :], in_=rows_side_by_side[:, M_SPLIT:, :])
+            nc.vector.tensor_copy(out=m_grouped[:, :M_SPLIT, :], in_=rows_side_by_side[:, :M_SPLIT, :])
             nc.vector.quantize_mx(
                 out=m_codes[:, half, :].bitcast(FP8X4),
                 scales=m_scales[:, half, :],
@@ -231,32 +259,23 @@ def tile_gcnnodeclassifiernetwork_pa_k_kernel(tc, A, x, W1_words, W1_scales, b1,
             )
 
         nc.vector.memset(w_planes[:].bitcast(I32), 0)
-        nc.vector.memset(bias_rows[:], 0.0)
-        nc.vector.memset(ones[:], 1.0)
         masks.make_identity(nc, ident[:])
-        nc.sync.dma_start(out=bias_rows[0:1, :], in_=b1.unsqueeze(0))
-        for g in range(HALVES):
-            nc.sync.dma_start(
-                out=a_raw[:, g], in_=A.rearrange("(g t p) j -> g p t j", t=PACK, p=P)[g]
-            )
+        nc.gpsimd.memset(bias_rows[:], 0.0)
+        nc.gpsimd.memset(ones[:], 1.0)
+        nc.gpsimd.memset(d[:], 1.0)
+        nc.scalar.activation(out=d[:, 0:1], in_=d[:, 0:1], func=ACT.Sqrt)
         for step in range(LOADS_AHEAD):
             load(step)
-        bias_bank = bank_pool.tile([P, HIDDEN], F32, tag="bank")
-        nc.tensor.matmul(out=bias_bank[:], lhsT=ones[:], rhs=bias_rows[:], start=True, stop=True)
-        nc.scalar.copy(out=bias_all[:], in_=bias_bank[:])
-        for piece in range(A_PIECES + 2):
-            if piece < A_PIECES:
-                regroup_a(piece)
-            if piece >= 2:
-                quantise_a(piece - 2)
-        column_sums = bank_pool.tile([P, ROW_TILES, DEG_COLS], F32, tag="bank")
-        sum_columns(column_sums)
+        nc.sync.dma_start(out=bias_rows[0:1, :], in_=b1.unsqueeze(0))
         sort_words(0)
-        normalisers(column_sums)
 
         for step in range(STEPS + 1):
             if step + LOADS_AHEAD < STEPS:
                 load(step + LOADS_AHEAD)
+            if step < HALVES:
+                nc.sync.dma_start(
+                    out=a_raw[:, step], in_=A.rearrange("(g t p) j -> g p t j", t=PACK, p=P)[step]
+                )
             if step + 1 < STEPS:
                 sort_words(step + 1)
             if step < STEPS:
@@ -268,25 +287,51 @@ def tile_gcnnodeclassifiernetwork_pa_k_kernel(tc, A, x, W1_words, W1_scales, b1,
                 half, chunk, first = place(step - 1)
                 if chunk == CHUNKS - 1:
                     empty_accumulators(step - 1)
-                    if first + TILES_PER_STEP == TILES_PER_HALF:
-                        quantise_m(half)
+            if step == SUMS_STEP:
+                bias_bank = bank_pool.tile([P, HIDDEN], F32, tag="bank")
+                nc.tensor.matmul(out=bias_bank[:], lhsT=ones[:], rhs=bias_rows[:], start=True, stop=True)
+                column_sums = bank_pool.tile([P, ROW_TILES, DEG_COLS], F32, tag="bank")
+                sum_columns(column_sums)
+                nc.scalar.copy(out=bias_all[:], in_=bias_bank[:])
+                normalisers(column_sums)
+            later = step - SUMS_STEP
+            if 0 <= later < A_PIECES // 2:
+                regroup_a(2 * later)
+                regroup_a(2 * later + 1)
+            if 1 <= later <= A_PIECES // 2:
+                quantise_a(2 * later - 2)
+                quantise_a(2 * later - 1)
+                scale_kept_h(later - 1)
+            if later == A_PIECES // 2 + 1:
+                quantise_m(0)
 
+        agg = {}
+
+        def aggregate(j, g):
+            if g == 0 and j < 4:
+                agg[j] = bank_pool.tile([P, HIDDEN], F32, name="agg", tag="bank")
+            elif g == 0:
+                agg[j] = acc_pool.tile([P, HIDDEN], F32, name="agg%d" % j, tag="acc%d" % (j - 4))
+            nc.tensor.matmul_mx(
+                out=agg[j][:],
+                lhsT=a_codes[:, g, j * P : (j + 1) * P].bitcast(FP8X4),
+                lhsT_scale=a_scales[:, g, j * P : (j + 1) * P],
+                rhs=m_codes[:, g, :].bitcast(FP8X4),
+                rhs_scale=m_scales[:, g, :],
+                start=(g == 0),
+                stop=(g == HALVES - 1),
+            )
+
+        for j in range(EARLY_TILES):
+            aggregate(j, 0)
         for j in range(ROW_TILES):
-            agg = bank_pool.tile([P, HIDDEN], F32, tag="bank")
-            for g in range(HALVES):
-                nc.tensor.matmul_mx(
-                    out=agg[:],
-                    lhsT=a_codes[:, g, j * P : (j + 1) * P].bitcast(FP8X4),
-                    lhsT_scale=a_scales[:, g, j * P : (j + 1) * P],
-                    rhs=m_codes[:, g, :].bitcast(FP8X4),
-                    rhs_scale=m_scales[:, g, :],
-                    start=(g == 0),
-                    stop=(g == HALVES - 1),
-                )
+            if j >= EARLY_TILES:
+                aggregate(j, 0)
+            aggregate(j, 1)
             result = out_pool.tile([P, HIDDEN], F32)
             nc.vector.scalar_tensor_tensor(
                 out=result[:],
-                in0=agg[:],
+                in0=agg[j][:],
                 scalar=d[:, j : j + 1],
                 in1=self_term[:, j, :],
                 op0=ALU.mult,

@@ -35,7 +35,7 @@ LOADS_AHEAD = 8
 DEG_COLS = 32
 A_PIECE = 256
 A_PIECES = HALVES * NODES // A_PIECE
-SUMS_STEP = 9
+SUMS_STEP = 10
 M_SPLIT = 336
 EARLY_TILES = 6
 A_BUFFERS = 4
@@ -272,9 +272,10 @@ def tile_gcnnodeclassifiernetwork_pa_k_kernel(tc, A, x, W1_words, W1_scales, b1,
         for step in range(STEPS + 1):
             if step + LOADS_AHEAD < STEPS:
                 load(step + LOADS_AHEAD)
-            if step < HALVES:
+            if 1 <= step <= HALVES:
+                g = step - 1
                 nc.sync.dma_start(
-                    out=a_raw[:, step], in_=A.rearrange("(g t p) j -> g p t j", t=PACK, p=P)[step]
+                    out=a_raw[:, g], in_=A.rearrange("(g t p) j -> g p t j", t=PACK, p=P)[g]
                 )
             if step + 1 < STEPS:
                 sort_words(step + 1)

@@ -35,8 +35,10 @@ LOADS_AHEAD = 8
 DEG_COLS = 32
 A_PIECE = 256
 A_PIECES = HALVES * NODES // A_PIECE
+A_STEP = 9
 SUMS_STEP = 10
-M_SPLIT = 336
+ALL_COLUMNS = slice(0, HIDDEN)
+COLUMN_HALVES = (slice(0, HIDDEN // 2), slice(HIDDEN // 2, HIDDEN))
 EARLY_TILES = 6
 A_BUFFERS = 4
 
@@ -79,6 +81,7 @@ def tile_gcnnodeclassifiernetwork_pa_k_kernel(tc, A, x, W1_words, W1_scales, b1,
         a_grouped = {}
         acc = {}
         m_rows = {}
+        m_grouped = {}
 
         def place(step):
             half, rest = divmod(step, STEPS_PER_HALF)
@@ -191,16 +194,26 @@ def tile_gcnnodeclassifiernetwork_pa_k_kernel(tc, A, x, W1_words, W1_scales, b1,
                 nc.scalar.copy(out=self_term[:, r0, :], in_=acc[first][:])
                 nc.vector.tensor_copy(out=self_term[:, r0 + 1, :], in_=acc[first + 1][:])
                 return
-            nc.scalar.activation(
-                out=m_rows[half][:, first, :], in_=acc[first][:], func=ACT.Copy, scale=d[:, r0 : r0 + 1]
-            )
-            self_from_acc(first)
-            nc.vector.tensor_scalar_mul(
-                out=m_rows[half][:, first + 1, :], in0=acc[first + 1][:], scalar1=d[:, r0 + 1 : r0 + 2]
-            )
-            if first + TILES_PER_STEP == TILES_PER_HALF:
-                quantise_m(half)
-            self_from_acc(first + 1)
+            tiles = range(first, first + TILES_PER_STEP)
+            for t in tiles:
+                r = half * TILES_PER_HALF + t
+                nc.scalar.activation(
+                    out=m_rows[half][:, t, :], in_=acc[t][:], func=ACT.Copy, scale=d[:, r : r + 1]
+                )
+            regroup_m(half, slice(first, first + TILES_PER_STEP))
+            if first == 0:
+                for t in tiles:
+                    self_from_acc(t)
+                return
+            quantise_m(half)
+            for t in tiles:
+                r = half * TILES_PER_HALF + t
+                nc.scalar.activation(
+                    out=self_term[:, r, :], in_=acc[t][:], func=ACT.Copy, scale=d_sq[:, r : r + 1]
+                )
+                nc.gpsimd.tensor_tensor(
+                    out=self_term[:, r, :], in0=self_term[:, r, :], in1=bias_all[:], op=ALU.add
+                )
 
         def self_from_acc(t):
             r = TILES_PER_HALF + t
@@ -226,16 +239,25 @@ def tile_gcnnodeclassifiernetwork_pa_k_kernel(tc, A, x, W1_words, W1_scales, b1,
                 op1=ALU.add,
             )
 
-        def quantise_m(half):
-            m_grouped = stage.tile([P, HIDDEN, PACK], BF16, align_bytes=64)
+        def regroup_m(half, tiles):
+            if tiles.start == 0:
+                m_grouped[half] = stage.tile([P, HIDDEN, PACK], BF16, name="m_grouped", align_bytes=64)
             rows_side_by_side = m_rows[half][:].rearrange("p t c -> p c t")
-            nc.scalar.copy(out=m_grouped[:, M_SPLIT:, :], in_=rows_side_by_side[:, M_SPLIT:, :])
-            nc.vector.tensor_copy(out=m_grouped[:, :M_SPLIT, :], in_=rows_side_by_side[:, :M_SPLIT, :])
-            nc.vector.quantize_mx(
-                out=m_codes[:, half, :].bitcast(FP8X4),
-                scales=m_scales[:, half, :],
-                in_=m_grouped[:].rearrange("p c t -> p (c t)"),
-            )
+            for cols in COLUMN_HALVES:
+                split = cols.start + (cols.stop - cols.start) * 21 // 32
+                for copy, part in (
+                    (nc.scalar.copy, slice(split, cols.stop)),
+                    (nc.vector.tensor_copy, slice(cols.start, split)),
+                ):
+                    copy(out=m_grouped[half][:, part, tiles], in_=rows_side_by_side[:, part, tiles])
+
+        def quantise_m(half):
+            for cols in COLUMN_HALVES:
+                nc.vector.quantize_mx(
+                    out=m_codes[:, half, cols].bitcast(FP8X4),
+                    scales=m_scales[:, half, cols],
+                    in_=m_grouped[half][:, cols, :].rearrange("p c t -> p (c t)"),
+                )
 
         def a_columns(piece):
             g, part = divmod(piece, A_PIECES // HALVES)
@@ -283,6 +305,8 @@ def tile_gcnnodeclassifiernetwork_pa_k_kernel(tc, A, x, W1_words, W1_scales, b1,
                 transpose(step)
             if step < STEPS:
                 quantise(step)
+            if step == STEPS - 1:
+                quantise_m(0)
             if step >= 1:
                 multiply(step - 1)
                 half, chunk, first = place(step - 1)
@@ -295,16 +319,17 @@ def tile_gcnnodeclassifiernetwork_pa_k_kernel(tc, A, x, W1_words, W1_scales, b1,
                 sum_columns(column_sums)
                 nc.scalar.copy(out=bias_all[:], in_=bias_bank[:])
                 normalisers(column_sums)
-            later = step - SUMS_STEP
+            later = step - A_STEP
             if 0 <= later < A_PIECES // 2:
                 regroup_a(2 * later)
                 regroup_a(2 * later + 1)
             if 1 <= later <= A_PIECES // 2:
                 quantise_a(2 * later - 2)
                 quantise_a(2 * later - 1)
-                scale_kept_h(later - 1)
-            if later == A_PIECES // 2 + 1:
-                quantise_m(0)
+            if 1 <= step - SUMS_STEP <= TILES_PER_HALF:
+                scale_kept_h(step - SUMS_STEP - 1)
+            if step - SUMS_STEP == TILES_PER_HALF:
+                regroup_m(0, slice(0, TILES_PER_HALF))
 
         agg = {}
 
@@ -330,13 +355,14 @@ def tile_gcnnodeclassifiernetwork_pa_k_kernel(tc, A, x, W1_words, W1_scales, b1,
                 aggregate(j, 0)
             aggregate(j, 1)
             result = out_pool.tile([P, HIDDEN], F32)
-            nc.vector.scalar_tensor_tensor(
-                out=result[:],
-                in0=agg[j][:],
-                scalar=d[:, j : j + 1],
-                in1=self_term[:, j, :],
-                op0=ALU.mult,
-                op1=ALU.add,
-            )
-            nc.scalar.activation(out=result[:], in_=result[:], func=ACT.Relu)
-            nc.sync.dma_start(out=out[j * P : (j + 1) * P, :], in_=result[:])
+            for cols in COLUMN_HALVES if j in (0, ROW_TILES - 1) else (ALL_COLUMNS,):
+                nc.vector.scalar_tensor_tensor(
+                    out=result[:, cols],
+                    in0=agg[j][:, cols],
+                    scalar=d[:, j : j + 1],
+                    in1=self_term[:, j, cols],
+                    op0=ALU.mult,
+                    op1=ALU.add,
+                )
+                nc.scalar.activation(out=result[:, cols], in_=result[:, cols], func=ACT.Relu)
+                nc.sync.dma_start(out=out[j * P : (j + 1) * P, cols], in_=result[:, cols])

@@ -23,20 +23,23 @@ ROW_TILES = NODES // P
 TILES_PER_HALF = PACK
 HALVES = ROW_TILES // TILES_PER_HALF
 TILES_PER_STEP = 2
-PASSES_PER_CHUNK = 4
-K_CHUNK = PASSES_PER_CHUNK * K_PASS
-CHUNKS = FEATURES // K_CHUNK
-STEPS_PER_CHUNK = TILES_PER_HALF // TILES_PER_STEP
-STEPS_PER_HALF = CHUNKS * STEPS_PER_CHUNK
-STEPS = HALVES * STEPS_PER_HALF
-WORDS_PER_PASS = K_PASS // 2
+PASSES = FEATURES // K_PASS
+PASSES_PER_PLANE = 4
+CHUNKS = (((0, 2), (2, 2), (4, 4), (8, 4), (12, 4)), ((0, 4), (4, 4), (8, 4), (12, 4)))
+STEPS = [
+    (half, first, count, tile)
+    for half in range(HALVES)
+    for first, count in CHUNKS[half]
+    for tile in range(0, TILES_PER_HALF, TILES_PER_STEP)
+]
 PASSES_PER_BANK = 2
 LOADS_AHEAD = 8
 DEG_COLS = 32
 A_PIECE = 256
 A_PIECES = HALVES * NODES // A_PIECE
-A_STEP = 9
-SUMS_STEP = 10
+A_LOADS = (11, 12)
+A_STEP = 11
+SUMS_STEP = 12
 ALL_COLUMNS = slice(0, HIDDEN)
 COLUMN_HALVES = (slice(0, HIDDEN // 2), slice(HIDDEN // 2, HIDDEN))
 EARLY_TILES = 6
@@ -57,8 +60,8 @@ def tile_gcnnodeclassifiernetwork_pa_k_kernel(tc, A, x, W1_words, W1_scales, b1,
         bank_pool = ctx.enter_context(tc.psum_pool(name="bank", bufs=4))
         ctx.enter_context(tc.manual_schedule())
 
-        w_words = keep.tile([P, CHUNKS * PASSES_PER_CHUNK, HIDDEN], U32, align_bytes=64)
-        w_planes = keep.tile([P, CHUNKS, HIDDEN], U8, align_bytes=64)
+        w_words = keep.tile([P, PASSES, HIDDEN], U32, align_bytes=64)
+        w_planes = keep.tile([P, PASSES // PASSES_PER_PLANE, HIDDEN], U8, align_bytes=64)
         a_raw = keep.tile([P, HALVES, PACK, NODES], BF16)
         a_codes = keep.tile([P, HALVES, NODES], U32, align_bytes=64)
         a_scales = keep.tile([P, HALVES, NODES], U8, align_bytes=64)
@@ -83,51 +86,53 @@ def tile_gcnnodeclassifiernetwork_pa_k_kernel(tc, A, x, W1_words, W1_scales, b1,
         m_rows = {}
         m_grouped = {}
 
-        def place(step):
-            half, rest = divmod(step, STEPS_PER_HALF)
-            chunk, pair = divmod(rest, STEPS_PER_CHUNK)
-            return half, chunk, pair * TILES_PER_STEP
-
         def load(step):
-            half, chunk, first = place(step)
-            x_tile = x_pool.tile([P, TILES_PER_STEP, K_CHUNK], BF16)
+            half, first, count, tile = STEPS[step]
+            x_tile = x_pool.tile([P, TILES_PER_STEP, count * K_PASS], BF16)
             x_tiles[step] = x_tile
             for t in range(TILES_PER_STEP):
-                row = (half * TILES_PER_HALF + first + t) * P
+                row = (half * TILES_PER_HALF + tile + t) * P
                 nc.sync.dma_start(
                     out=x_tile[:, t, :],
-                    in_=x[row : row + P, chunk * K_CHUNK : (chunk + 1) * K_CHUNK],
+                    in_=x[row : row + P, first * K_PASS : (first + count) * K_PASS],
                 )
-            if half == 0 and first + TILES_PER_STEP == TILES_PER_HALF:
-                passes = slice(chunk * PASSES_PER_CHUNK, (chunk + 1) * PASSES_PER_CHUNK)
-                for quad in range(4):
-                    nc.sync.dma_start(
-                        out=w_planes[32 * quad : 32 * quad + 16, chunk, :].bitcast(I32),
-                        in_=W1_scales[passes, 4 * quad : 4 * quad + 4, :].bitcast(I32),
-                    )
+            if half == 0 and tile + TILES_PER_STEP == TILES_PER_HALF:
+                if first % PASSES_PER_PLANE == 0:
+                    passes = slice(first, first + PASSES_PER_PLANE)
+                    for quad in range(4):
+                        nc.sync.dma_start(
+                            out=w_planes[32 * quad : 32 * quad + 16, first // PASSES_PER_PLANE, :].bitcast(I32),
+                            in_=W1_scales[passes, 4 * quad : 4 * quad + 4, :].bitcast(I32),
+                        )
+                passes = slice(first, first + count)
                 nc.sync.dma_start(
                     out=w_words[:, passes, :].bitcast(I32),
                     in_=W1_words[passes].rearrange("g p n t -> p g (n t)").bitcast(I32),
                 )
+            if step in A_LOADS:
+                g = A_LOADS.index(step)
+                nc.sync.dma_start(
+                    out=a_raw[:, g], in_=A.rearrange("(g t p) j -> g p t j", t=PACK, p=P)[g]
+                )
 
         def sort_words(step):
-            words = stage.tile([P, TILES_PER_STEP, PASSES_PER_CHUNK, 2, P], F32)
+            count = STEPS[step][2]
+            words = stage.tile([P, TILES_PER_STEP, count, 2, P], F32)
             sorted_tiles[step] = words
             for t in range(TILES_PER_STEP):
                 nc.vector.tensor_copy(
                     out=words[:, t],
                     in_=x_tiles[step][:, t, :]
                     .bitcast(F32)
-                    .rearrange("p (g q u) -> p g u q", g=PASSES_PER_CHUNK, u=2),
+                    .rearrange("p (g q u) -> p g u q", g=count, u=2),
                 )
 
         def transpose(step):
-            grouped = stage.tile(
-                [P, TILES_PER_STEP, PASSES_PER_CHUNK, P, PACK], BF16, align_bytes=64
-            )
+            count = STEPS[step][2]
+            grouped = stage.tile([P, TILES_PER_STEP, count, P, PACK], BF16, align_bytes=64)
             grouped_tiles[step] = grouped
             for t in range(TILES_PER_STEP):
-                for g0 in range(0, PASSES_PER_CHUNK, PASSES_PER_BANK):
+                for g0 in range(0, count, PASSES_PER_BANK):
                     flipped = bank_pool.tile([P, PASSES_PER_BANK, 2, P], F32, tag="bank")
                     for g in range(PASSES_PER_BANK):
                         for u in range(2):
@@ -140,8 +145,9 @@ def tile_gcnnodeclassifiernetwork_pa_k_kernel(tc, A, x, W1_words, W1_scales, b1,
                     )
 
         def quantise(step):
-            codes = stage.tile([P, TILES_PER_STEP, PASSES_PER_CHUNK, P], U32, align_bytes=64)
-            scales = stage.tile([P, TILES_PER_STEP, PASSES_PER_CHUNK, P], U8, align_bytes=64)
+            count = STEPS[step][2]
+            codes = stage.tile([P, TILES_PER_STEP, count, P], U32, align_bytes=64)
+            scales = stage.tile([P, TILES_PER_STEP, count, P], U8, align_bytes=64)
             x_codes[step] = codes
             x_scales[step] = scales
             for t in range(TILES_PER_STEP):
@@ -152,21 +158,22 @@ def tile_gcnnodeclassifiernetwork_pa_k_kernel(tc, A, x, W1_words, W1_scales, b1,
                 )
 
         def multiply(step):
-            half, chunk, first = place(step)
+            half, first, count, tile = STEPS[step]
             for t in range(TILES_PER_STEP):
-                if chunk == 0:
-                    acc[first + t] = acc_pool.tile(
-                        [P, HIDDEN], F32, name="acc%d" % (first + t), tag="acc%d" % (first + t)
+                if first == 0:
+                    acc[tile + t] = acc_pool.tile(
+                        [P, HIDDEN], F32, name="acc%d" % (tile + t), tag="acc%d" % (tile + t)
                     )
-                for o in range(PASSES_PER_CHUNK):
+                for o in range(count):
+                    g = first + o
                     nc.tensor.matmul_mx(
-                        out=acc[first + t][:],
+                        out=acc[tile + t][:],
                         lhsT=x_codes[step][:, t, o, :].bitcast(FP8X4),
                         lhsT_scale=x_scales[step][:, t, o, :],
-                        rhs=w_words[:, chunk * PASSES_PER_CHUNK + o, :].bitcast(FP8X4),
-                        rhs_scale=w_planes[4 * o : P, chunk, :],
-                        start=(chunk == 0 and o == 0),
-                        stop=(chunk == CHUNKS - 1 and o == PASSES_PER_CHUNK - 1),
+                        rhs=w_words[:, g, :].bitcast(FP8X4),
+                        rhs_scale=w_planes[PACK * (g % PASSES_PER_PLANE) : P, g // PASSES_PER_PLANE, :],
+                        start=(g == 0),
+                        stop=(g == PASSES - 1),
                     )
 
         def sum_columns(sums):
@@ -186,7 +193,7 @@ def tile_gcnnodeclassifiernetwork_pa_k_kernel(tc, A, x, W1_words, W1_scales, b1,
             nc.scalar.activation(out=d[:], in_=d_sq[:], func=ACT.Sqrt)
 
         def empty_accumulators(step):
-            half, chunk, first = place(step)
+            half, first = STEPS[step][0], STEPS[step][3]
             if first == 0:
                 m_rows[half] = stage.tile([P, TILES_PER_HALF, HIDDEN], BF16, name="m_rows")
             r0 = half * TILES_PER_HALF + first
@@ -197,9 +204,13 @@ def tile_gcnnodeclassifiernetwork_pa_k_kernel(tc, A, x, W1_words, W1_scales, b1,
             tiles = range(first, first + TILES_PER_STEP)
             for t in tiles:
                 r = half * TILES_PER_HALF + t
-                nc.scalar.activation(
-                    out=m_rows[half][:, t, :], in_=acc[t][:], func=ACT.Copy, scale=d[:, r : r + 1]
-                )
+                for cols in COLUMN_HALVES if t == TILES_PER_HALF - 1 else (ALL_COLUMNS,):
+                    nc.scalar.activation(
+                        out=m_rows[half][:, t, cols],
+                        in_=acc[t][:, cols],
+                        func=ACT.Copy,
+                        scale=d[:, r : r + 1],
+                    )
             regroup_m(half, slice(first, first + TILES_PER_STEP))
             if first == 0:
                 for t in tiles:
@@ -291,26 +302,19 @@ def tile_gcnnodeclassifiernetwork_pa_k_kernel(tc, A, x, W1_words, W1_scales, b1,
         nc.sync.dma_start(out=bias_rows[0:1, :], in_=b1.unsqueeze(0))
         sort_words(0)
 
-        for step in range(STEPS + 1):
-            if step + LOADS_AHEAD < STEPS:
+        for step in range(len(STEPS) + 1):
+            if step + LOADS_AHEAD < len(STEPS):
                 load(step + LOADS_AHEAD)
-            if 1 <= step <= HALVES:
-                g = step - 1
-                nc.sync.dma_start(
-                    out=a_raw[:, g], in_=A.rearrange("(g t p) j -> g p t j", t=PACK, p=P)[g]
-                )
-            if step + 1 < STEPS:
+            if step + 1 < len(STEPS):
                 sort_words(step + 1)
-            if step < STEPS:
+            if step < len(STEPS):
                 transpose(step)
-            if step < STEPS:
                 quantise(step)
-            if step == STEPS - 1:
+            if step == len(STEPS) - 1:
                 quantise_m(0)
             if step >= 1:
                 multiply(step - 1)
-                half, chunk, first = place(step - 1)
-                if chunk == CHUNKS - 1:
+                if STEPS[step - 1][1] + STEPS[step - 1][2] == PASSES:
                     empty_accumulators(step - 1)
             if step == SUMS_STEP:
                 bias_bank = bank_pool.tile([P, HIDDEN], F32, tag="bank")
@@ -364,5 +368,8 @@ def tile_gcnnodeclassifiernetwork_pa_k_kernel(tc, A, x, W1_words, W1_scales, b1,
                     op0=ALU.mult,
                     op1=ALU.add,
                 )
-                nc.scalar.activation(out=result[:, cols], in_=result[:, cols], func=ACT.Relu)
+                if j == ROW_TILES - 1:
+                    nc.vector.tensor_scalar_max(out=result[:, cols], in0=result[:, cols], scalar1=0.0)
+                else:
+                    nc.scalar.activation(out=result[:, cols], in_=result[:, cols], func=ACT.Relu)
                 nc.sync.dma_start(out=out[j * P : (j + 1) * P, cols], in_=result[:, cols])

@@ -37,9 +37,10 @@ LOADS_AHEAD = 8
 DEG_COLS = 32
 A_PIECE = 256
 A_PIECES = HALVES * NODES // A_PIECE
-A_LOADS = (11, 12)
+A_LOADS = (11, 13)
 A_STEP = 11
-SUMS_STEP = 12
+SUMS_STEP = 13
+KEPT_TILES = ((), (0,), (1, 2), (3,))
 ALL_COLUMNS = slice(0, HIDDEN)
 COLUMN_HALVES = (slice(0, HIDDEN // 2), slice(HIDDEN // 2, HIDDEN))
 EARLY_TILES = 6
@@ -330,9 +331,10 @@ def tile_gcnnodeclassifiernetwork_pa_k_kernel(tc, A, x, W1_words, W1_scales, b1,
             if 1 <= later <= A_PIECES // 2:
                 quantise_a(2 * later - 2)
                 quantise_a(2 * later - 1)
-            if 1 <= step - SUMS_STEP <= TILES_PER_HALF:
-                scale_kept_h(step - SUMS_STEP - 1)
-            if step - SUMS_STEP == TILES_PER_HALF:
+            if 0 <= step - SUMS_STEP < len(KEPT_TILES):
+                for r in KEPT_TILES[step - SUMS_STEP]:
+                    scale_kept_h(r)
+            if step - SUMS_STEP == len(KEPT_TILES) - 1:
                 regroup_m(0, slice(0, TILES_PER_HALF))
 
         agg = {}

from contextlib import ExitStack

import concourse.masks as masks
import concourse.mybir as mybir

F32 = mybir.dt.float32
BF16 = mybir.dt.bfloat16
I32 = mybir.dt.int32
U32 = mybir.dt.uint32
U8 = mybir.dt.uint8
FP8X4 = mybir.dt.float8_e4m3fn_x4
ACT = mybir.ActivationFunctionType
ALU = mybir.AluOpType

P = 128
PACK = 4
K_PASS = P * PACK
NODES = 1024
FEATURES = 8192
HIDDEN = 512

ROW_TILES = NODES // P
TILES_PER_HALF = PACK
HALVES = ROW_TILES // TILES_PER_HALF
TILES_PER_STEP = 2
PASSES = FEATURES // K_PASS
PASSES_PER_PLANE = 4
CHUNKS = (((0, 2), (2, 2), (4, 4), (8, 4), (12, 4)), ((0, 4), (4, 4), (8, 4), (12, 4)))
STEPS = [
    (half, first, count, tile)
    for half in range(HALVES)
    for first, count in CHUNKS[half]
    for tile in range(0, TILES_PER_HALF, TILES_PER_STEP)
]
PASSES_PER_BANK = 2
LOADS_AHEAD = 8
DEG_COLS = 32
A_PIECE = 256
A_PIECES = HALVES * NODES // A_PIECE
A_LOADS = (11, 13)
A_STEP = 11
SUMS_STEP = 13
KEPT_TILES = ((), (0,), (1, 2), (3,))
ALL_COLUMNS = slice(0, HIDDEN)
COLUMN_HALVES = (slice(0, HIDDEN // 2), slice(HIDDEN // 2, HIDDEN))
EARLY_TILES = 6
A_BUFFERS = 4

FLOPS = 2 * NODES * FEATURES * HIDDEN + 2 * NODES * NODES * HIDDEN


def tile_gcnnodeclassifiernetwork_pa_k_kernel(tc, A, x, W1_words, W1_scales, b1, out):
    nc = tc.nc
    with ExitStack() as ctx:
        keep = ctx.enter_context(tc.tile_pool(name="keep", bufs=1))
        x_pool = ctx.enter_context(tc.tile_pool(name="x", bufs=LOADS_AHEAD))
        stage = ctx.enter_context(tc.tile_pool(name="stage", bufs=2))
        a_pool = ctx.enter_context(tc.tile_pool(name="a", bufs=A_BUFFERS))
        out_pool = ctx.enter_context(tc.tile_pool(name="out", bufs=ROW_TILES))
        acc_pool = ctx.enter_context(tc.psum_pool(name="acc", bufs=1))
        bank_pool = ctx.enter_context(tc.psum_pool(name="bank", bufs=4))
        ctx.enter_context(tc.manual_schedule())

        w_words = keep.tile([P, PASSES, HIDDEN], U32, align_bytes=64)
        w_planes = keep.tile([P, PASSES // PASSES_PER_PLANE, HIDDEN], U8, align_bytes=64)
        a_raw = keep.tile([P, HALVES, PACK, NODES], BF16)
        a_codes = keep.tile([P, HALVES, NODES], U32, align_bytes=64)
        a_scales = keep.tile([P, HALVES, NODES], U8, align_bytes=64)
        m_codes = keep.tile([P, HALVES, HIDDEN], U32, align_bytes=64)
        m_scales = keep.tile([P, HALVES, HIDDEN], U8, align_bytes=64)
        self_term = keep.tile([P, ROW_TILES, HIDDEN], F32)
        bias_all = keep.tile([P, HIDDEN], F32)
        bias_rows = keep.tile([P, HIDDEN], BF16)
        ones = keep.tile([P, P], BF16)
        ident = keep.tile([P, P], F32)
        deg = keep.tile([P, ROW_TILES], F32)
        d_sq = keep.tile([P, ROW_TILES], F32)
        d = keep.tile([P, ROW_TILES], F32)

        x_tiles = {}
        sorted_tiles = {}
        grouped_tiles = {}
        x_codes = {}
        x_scales = {}
        a_grouped = {}
        acc = {}
        m_rows = {}
        m_grouped = {}

        def load(step):
            half, first, count, tile = STEPS[step]
            x_tile = x_pool.tile([P, TILES_PER_STEP, count * K_PASS], BF16)
            x_tiles[step] = x_tile
            for t in range(TILES_PER_STEP):
                row = (half * TILES_PER_HALF + tile + t) * P
                nc.sync.dma_start(
                    out=x_tile[:, t, :],
                    in_=x[row : row + P, first * K_PASS : (first + count) * K_PASS],
                )
            if half == 0 and tile + TILES_PER_STEP == TILES_PER_HALF:
                if first % PASSES_PER_PLANE == 0:
                    passes = slice(first, first + PASSES_PER_PLANE)
                    for quad in range(4):
                        nc.sync.dma_start(
                            out=w_planes[32 * quad : 32 * quad + 16, first // PASSES_PER_PLANE, :].bitcast(I32),
                            in_=W1_scales[passes, 4 * quad : 4 * quad + 4, :].bitcast(I32),
                        )
                passes = slice(first, first + count)
                nc.sync.dma_start(
                    out=w_words[:, passes, :].bitcast(I32),
                    in_=W1_words[passes].rearrange("g p n t -> p g (n t)").bitcast(I32),
                )
            if step in A_LOADS:
                g = A_LOADS.index(step)
                nc.sync.dma_start(
                    out=a_raw[:, g], in_=A.rearrange("(g t p) j -> g p t j", t=PACK, p=P)[g]
                )

        def sort_words(step):
            count = STEPS[step][2]
            words = stage.tile([P, TILES_PER_STEP, count, 2, P], F32)
            sorted_tiles[step] = words
            for t in range(TILES_PER_STEP):
                nc.vector.tensor_copy(
                    out=words[:, t],
                    in_=x_tiles[step][:, t, :]
                    .bitcast(F32)
                    .rearrange("p (g q u) -> p g u q", g=count, u=2),
                )

        def transpose(step):
            count = STEPS[step][2]
            grouped = stage.tile([P, TILES_PER_STEP, count, P, PACK], BF16, align_bytes=64)
            grouped_tiles[step] = grouped
            for t in range(TILES_PER_STEP):
                for g0 in range(0, count, PASSES_PER_BANK):
                    flipped = bank_pool.tile([P, PASSES_PER_BANK, 2, P], F32, tag="bank")
                    for g in range(PASSES_PER_BANK):
                        for u in range(2):
                            nc.tensor.transpose(
                                flipped[:, g, u, :], sorted_tiles[step][:, t, g0 + g, u, :], ident[:]
                            )
                    nc.scalar.copy(
                        out=grouped[:, t, g0 : g0 + PASSES_PER_BANK].bitcast(F32),
                        in_=flipped[:].rearrange("p g u r -> p g r u"),
                    )

        def quantise(step):
            count = STEPS[step][2]
            codes = stage.tile([P, TILES_PER_STEP, count, P], U32, align_bytes=64)
            scales = stage.tile([P, TILES_PER_STEP, count, P], U8, align_bytes=64)
            x_codes[step] = codes
            x_scales[step] = scales
            for t in range(TILES_PER_STEP):
                nc.vector.quantize_mx(
                    out=codes[:, t].rearrange("p g r -> p (g r)").bitcast(FP8X4),
                    scales=scales[:, t].rearrange("p g r -> p (g r)"),
                    in_=grouped_tiles[step][:, t].rearrange("p g r k -> p (g r k)"),
                )

        def multiply(step):
            half, first, count, tile = STEPS[step]
            for t in range(TILES_PER_STEP):
                if first == 0:
                    acc[tile + t] = acc_pool.tile(
                        [P, HIDDEN], F32, name="acc%d" % (tile + t), tag="acc%d" % (tile + t)
                    )
                for o in range(count):
                    g = first + o
                    nc.tensor.matmul_mx(
                        out=acc[tile + t][:],
                        lhsT=x_codes[step][:, t, o, :].bitcast(FP8X4),
                        lhsT_scale=x_scales[step][:, t, o, :],
                        rhs=w_words[:, g, :].bitcast(FP8X4),
                        rhs_scale=w_planes[PACK * (g % PASSES_PER_PLANE) : P, g // PASSES_PER_PLANE, :],
                        start=(g == 0),
                        stop=(g == PASSES - 1),
                    )

        def sum_columns(sums):
            for j in range(ROW_TILES):
                for i in range(ROW_TILES):
                    nc.tensor.matmul(
                        out=sums[:, j, :],
                        lhsT=a_raw[:, i // PACK, i % PACK, j * P : (j + 1) * P],
                        rhs=ones[:, :DEG_COLS],
                        start=(i == 0),
                        stop=(i == ROW_TILES - 1),
                    )

        def normalisers(sums):
            nc.vector.tensor_scalar_add(out=deg[:], in0=sums[:, :, 0], scalar1=1.0)
            nc.vector.reciprocal(out=d_sq[:], in_=deg[:])
            nc.scalar.activation(out=d[:], in_=d_sq[:], func=ACT.Sqrt)

        def empty_accumulators(step):
            half, first = STEPS[step][0], STEPS[step][3]
            if first == 0:
                m_rows[half] = stage.tile([P, TILES_PER_HALF, HIDDEN], BF16, name="m_rows")
            r0 = half * TILES_PER_HALF + first
            if half == 0:
                nc.scalar.copy(out=self_term[:, r0, :], in_=acc[first][:])
                nc.vector.tensor_copy(out=self_term[:, r0 + 1, :], in_=acc[first + 1][:])
                return
            tiles = range(first, first + TILES_PER_STEP)
            for t in tiles:
                r = half * TILES_PER_HALF + t
                for cols in COLUMN_HALVES if t == TILES_PER_HALF - 1 else (ALL_COLUMNS,):
                    nc.scalar.activation(
                        out=m_rows[half][:, t, cols],
                        in_=acc[t][:, cols],
                        func=ACT.Copy,
                        scale=d[:, r : r + 1],
                    )
            regroup_m(half, slice(first, first + TILES_PER_STEP))
            if first == 0:
                for t in tiles:
                    self_from_acc(t)
                return
            quantise_m(half)
            for t in tiles:
                r = half * TILES_PER_HALF + t
                nc.scalar.activation(
                    out=self_term[:, r, :], in_=acc[t][:], func=ACT.Copy, scale=d_sq[:, r : r + 1]
                )
                nc.gpsimd.tensor_tensor(
                    out=self_term[:, r, :], in0=self_term[:, r, :], in1=bias_all[:], op=ALU.add
                )

        def self_from_acc(t):
            r = TILES_PER_HALF + t
            nc.vector.scalar_tensor_tensor(
                out=self_term[:, r, :],
                in0=acc[t][:],
                scalar=d_sq[:, r : r + 1],
                in1=bias_all[:],
                op0=ALU.mult,
                op1=ALU.add,
            )

        def scale_kept_h(r):
            nc.scalar.activation(
                out=m_rows[0][:, r, :], in_=self_term[:, r, :], func=ACT.Copy, scale=d[:, r : r + 1]
            )
            nc.vector.scalar_tensor_tensor(
                out=self_term[:, r, :],
                in0=self_term[:, r, :],
                scalar=d_sq[:, r : r + 1],
                in1=bias_all[:],
                op0=ALU.mult,
                op1=ALU.add,
            )

        def regroup_m(half, tiles):
            if tiles.start == 0:
                m_grouped[half] = stage.tile([P, HIDDEN, PACK], BF16, name="m_grouped", align_bytes=64)
            rows_side_by_side = m_rows[half][:].rearrange("p t c -> p c t")
            for cols in COLUMN_HALVES:
                split = cols.start + (cols.stop - cols.start) * 21 // 32
                for copy, part in (
                    (nc.scalar.copy, slice(split, cols.stop)),
                    (nc.vector.tensor_copy, slice(cols.start, split)),
                ):
                    copy(out=m_grouped[half][:, part, tiles], in_=rows_side_by_side[:, part, tiles])

        def quantise_m(half):
            for cols in COLUMN_HALVES:
                nc.vector.quantize_mx(
                    out=m_codes[:, half, cols].bitcast(FP8X4),
                    scales=m_scales[:, half, cols],
                    in_=m_grouped[half][:, cols, :].rearrange("p c t -> p (c t)"),
                )

        def a_columns(piece):
            g, part = divmod(piece, A_PIECES // HALVES)
            return g, slice(part * A_PIECE, (part + 1) * A_PIECE)

        def regroup_a(piece):
            g, cols = a_columns(piece)
            a_grouped[piece] = a_pool.tile([P, A_PIECE, PACK], BF16, name="a_grouped", align_bytes=64)
            rows_side_by_side = a_raw[:, g, :, cols].rearrange("p t j -> p j t")
            if piece % 2 == 0:
                nc.vector.tensor_copy(out=a_grouped[piece][:], in_=rows_side_by_side)
            else:
                nc.scalar.copy(out=a_grouped[piece][:], in_=rows_side_by_side)

        def quantise_a(piece):
            g, cols = a_columns(piece)
            nc.vector.quantize_mx(
                out=a_codes[:, g, cols].bitcast(FP8X4),
                scales=a_scales[:, g, cols],
                in_=a_grouped[piece][:].rearrange("p j t -> p (j t)"),
            )

        nc.vector.memset(w_planes[:].bitcast(I32), 0)
        masks.make_identity(nc, ident[:])
        nc.gpsimd.memset(bias_rows[:], 0.0)
        nc.gpsimd.memset(ones[:], 1.0)
        nc.gpsimd.memset(d[:], 1.0)
        nc.scalar.activation(out=d[:, 0:1], in_=d[:, 0:1], func=ACT.Sqrt)
        for step in range(LOADS_AHEAD):
            load(step)
        nc.sync.dma_start(out=bias_rows[0:1, :], in_=b1.unsqueeze(0))
        sort_words(0)

        for step in range(len(STEPS) + 1):
            if step + LOADS_AHEAD < len(STEPS):
                load(step + LOADS_AHEAD)
            if step + 1 < len(STEPS):
                sort_words(step + 1)
            if step < len(STEPS):
                transpose(step)
                quantise(step)
            if step == len(STEPS) - 1:
                quantise_m(0)
            if step >= 1:
                multiply(step - 1)
                if STEPS[step - 1][1] + STEPS[step - 1][2] == PASSES:
                    empty_accumulators(step - 1)
            if step == SUMS_STEP:
                bias_bank = bank_pool.tile([P, HIDDEN], F32, tag="bank")
                nc.tensor.matmul(out=bias_bank[:], lhsT=ones[:], rhs=bias_rows[:], start=True, stop=True)
                column_sums = bank_pool.tile([P, ROW_TILES, DEG_COLS], F32, tag="bank")
                sum_columns(column_sums)
                nc.scalar.copy(out=bias_all[:], in_=bias_bank[:])
                normalisers(column_sums)
            later = step - A_STEP
            if 0 <= later < A_PIECES // 2:
                regroup_a(2 * later)
                regroup_a(2 * later + 1)
            if 1 <= later <= A_PIECES // 2:
                quantise_a(2 * later - 2)
                quantise_a(2 * later - 1)
            if 0 <= step - SUMS_STEP < len(KEPT_TILES):
                for r in KEPT_TILES[step - SUMS_STEP]:
                    scale_kept_h(r)
            if step - SUMS_STEP == len(KEPT_TILES) - 1:
                regroup_m(0, slice(0, TILES_PER_HALF))

        agg = {}

        def aggregate(j, g):
            if g == 0 and j < 4:
                agg[j] = bank_pool.tile([P, HIDDEN], F32, name="agg", tag="bank")
            elif g == 0:
                agg[j] = acc_pool.tile([P, HIDDEN], F32, name="agg%d" % j, tag="acc%d" % (j - 4))
            nc.tensor.matmul_mx(
                out=agg[j][:],
                lhsT=a_codes[:, g, j * P : (j + 1) * P].bitcast(FP8X4),
                lhsT_scale=a_scales[:, g, j * P : (j + 1) * P],
                rhs=m_codes[:, g, :].bitcast(FP8X4),
                rhs_scale=m_scales[:, g, :],
                start=(g == 0),
                stop=(g == HALVES - 1),
            )

        for j in range(EARLY_TILES):
            aggregate(j, 0)
        for j in range(ROW_TILES):
            if j >= EARLY_TILES:
                aggregate(j, 0)
            aggregate(j, 1)
            result = out_pool.tile([P, HIDDEN], F32)
            for cols in COLUMN_HALVES if j in (0, ROW_TILES - 1) else (ALL_COLUMNS,):
                nc.vector.scalar_tensor_tensor(
                    out=result[:, cols],
                    in0=agg[j][:, cols],
                    scalar=d[:, j : j + 1],
                    in1=self_term[:, j, cols],
                    op0=ALU.mult,
                    op1=ALU.add,
                )
                if j == ROW_TILES - 1:
                    nc.vector.tensor_scalar_max(out=result[:, cols], in0=result[:, cols], scalar1=0.0)
                else:
                    nc.scalar.activation(out=result[:, cols], in_=result[:, cols], func=ACT.Relu)
                nc.sync.dma_start(out=out[j * P : (j + 1) * P, cols], in_=result[:, cols])
